import numpy as np
import ml_dtypes

BF16 = ml_dtypes.bfloat16


def bf(x):
    return np.asarray(x, np.float32).astype(BF16)


def f32(x):
    return np.asarray(x, np.float32)


def f64(x):
    return np.asarray(x).astype(np.float64)


def striped(idx):
    return np.tile(idx.reshape(-1, 16).T, (8, 1))


H, S, SL, B, N = 128, 1024, 8, 256, 2048


def setup_inputs():
    return {
        "table": bf(np.random.standard_normal((H, S))),
        "w": bf(np.random.standard_normal((H, H)) / np.sqrt(H)),
        "query": bf(np.random.standard_normal((H, B))),
        "sim_q": bf(np.random.standard_normal((H, 1)) / np.sqrt(H)),
        "sim_k": bf(np.random.standard_normal((H, 1)) / np.sqrt(H)),
        "sim_b": f32(0.5 + 0.1 * np.random.standard_normal((1,))),
        "offs": striped(np.random.permutation(np.tile(np.arange(S), 2))[:N]),
    }


def reference(table, w, query, sim_q, sim_k, sim_b, offs):
    idx = offs[:16].T.reshape(-1)
    kv = (f64(w).T @ f64(table)[:, idx]).reshape(H, SL, B)
    q = f64(w).T @ f64(query)
    qs = f64(sim_q)[:, 0] @ q
    ks = np.tensordot(f64(sim_k)[:, 0], kv, axes=(0, 0))
    logit = np.maximum(qs[None, :] + ks + f64(sim_b)[0], 0.0)
    e = np.exp(logit - logit.max(axis=0, keepdims=True))
    score = e / e.sum(axis=0, keepdims=True)
    return (score[None, :, :] * kv).sum(axis=1)

@@ -1,0 +1,126 @@
+import concourse.mybir as mybir
+from concourse.masks import make_identity
+
+BF16, F32, U16 = mybir.dt.bfloat16, mybir.dt.float32, mybir.dt.uint16
+ALU = mybir.AluOpType
+FUNC = mybir.ActivationFunctionType
+X = mybir.AxisListType.X
+
+P = 128
+S = 1024
+SLOTS = 8
+B = 256
+N = SLOTS * B
+HALVES = B // P
+PIECE = 512
+PIECES = N // PIECE
+BLOCKS = PIECE // P
+
+FLOPS = 2 * P * P * (N + B) + 2 * P * (N + B) + 2 * P * N
+
+
+def tile_memory_kernel(tc, table, w, query, sim_q, sim_k, sim_b, offs, out):
+    nc = tc.nc
+    with (
+        tc.tile_pool(name="held", bufs=1) as held,
+        tc.psum_pool(name="kv_banks", bufs=PIECES) as kv_banks,
+        tc.psum_pool(name="small_banks", bufs=1) as small_banks,
+    ):
+        offsets = held.tile([P, N // 16], U16, name="offsets")
+        nc.sync.dma_start(offsets[:], offs)
+        table_sb = held.tile([P, S], BF16, name="table_sb")
+        nc.scalar.dma_start(table_sb[:], table)
+        w_sb = held.tile([P, P], BF16, name="w_sb")
+        nc.sync.dma_start(w_sb[:], w)
+        query_sb = held.tile([P, B], BF16, name="query_sb")
+        nc.sync.dma_start(query_sb[:], query)
+        simk_sb = held.tile([P, 1], BF16, name="simk_sb")
+        nc.scalar.dma_start(simk_sb[:], sim_k)
+        simq_sb = held.tile([P, 1], BF16, name="simq_sb")
+        nc.scalar.dma_start(simq_sb[:], sim_q)
+        bias_sb = held.tile([P, 1], F32, name="bias_sb")
+        nc.sync.dma_start(bias_sb[:], sim_b.partition_broadcast(P))
+
+        warm = held.tile([P, 1], F32, name="warm")
+        nc.vector.memset(warm[:], 0.0)
+        nc.scalar.activation(warm[:], warm[:], FUNC.Exp)
+
+        ident = held.tile([P, P], F32, name="ident")
+        make_identity(nc, ident[:])
+
+        logit_ps = small_banks.tile([P, HALVES * SLOTS + HALVES], F32, name="logit_ps")
+
+        kv_ps = []
+        for p in range(PIECES):
+            kv_ps.append(kv_banks.tile([P, PIECE], F32, name=f"kv_ps{p}", tag="bank"))
+            piece_offsets = offsets[:, p * (PIECE // 16) : (p + 1) * (PIECE // 16)]
+            nc.tensor.matmul(kv_ps[p][:], w_sb[:], table_sb[:].indirect(piece_offsets), start=True, stop=True)
+
+        q_ps = small_banks.tile([P, B], F32, name="q_ps", tag="wide")
+        nc.tensor.matmul(q_ps[:], w_sb[:], query_sb[:], start=True, stop=True)
+        q_bf = held.tile([P, B], BF16, name="q_bf")
+        nc.vector.tensor_copy(q_bf[:], q_ps[:])
+        for h in range(HALVES):
+            col = HALVES * SLOTS + h
+            nc.tensor.matmul(
+                logit_ps[:, col : col + 1], q_bf[:, h * P : (h + 1) * P], simq_sb[:], start=True, stop=True
+            )
+        q_term = held.tile([P, HALVES], F32, name="q_term")
+        nc.vector.tensor_scalar(q_term[:], logit_ps[:, HALVES * SLOTS :], bias_sb[:, 0:1], None, op0=ALU.add)
+
+        kvT_ps = []
+        for p in range(PIECES):
+            kv_bf = held.tile([P, PIECE], BF16, name=f"kv_bf{p}")
+            nc.scalar.activation(kv_bf[:], kv_ps[p][:], FUNC.Copy)
+            kv_sb = held.tile([P, PIECE], F32, name=f"kv_sb{p}")
+            nc.vector.tensor_copy(kv_sb[:], kv_ps[p][:])
+            kvT_ps.append(kv_banks.tile([P, BLOCKS, P], F32, name=f"kvT_ps{p}", tag="bank"))
+            for b in range(BLOCKS):
+                t, h = divmod(p * BLOCKS + b, HALVES)
+                col = h * SLOTS + t
+                block = slice(b * P, (b + 1) * P)
+                nc.tensor.matmul(logit_ps[:, col : col + 1], kv_bf[:, block], simk_sb[:], start=True, stop=True)
+                nc.tensor.transpose(kvT_ps[p][:, b, :], kv_sb[:, block], ident[:])
+
+        logit = held.tile([P, HALVES, SLOTS], F32, name="logit")
+        for h in range(HALVES):
+            nc.vector.tensor_scalar(
+                logit[:, h, :],
+                logit_ps[:, h * SLOTS : (h + 1) * SLOTS],
+                q_term[:, h : h + 1],
+                0.0,
+                op0=ALU.add,
+                op1=ALU.max,
+            )
+        per_slot = [P, HALVES, SLOTS]
+        top = held.tile([P, HALVES], F32, name="top")
+        nc.vector.tensor_reduce(top[:], logit[:], axis=X, op=ALU.max)
+        shifted = held.tile(per_slot, F32, name="shifted")
+        nc.vector.tensor_tensor(shifted[:], logit[:], top[:].unsqueeze(2).to_broadcast(per_slot), ALU.subtract)
+        expd = held.tile(per_slot, F32, name="expd")
+        nc.scalar.activation(expd[:], shifted[:], FUNC.Exp)
+        total = held.tile([P, HALVES], F32, name="total")
+        nc.vector.tensor_reduce(total[:], expd[:], axis=X, op=ALU.add)
+        inv_total = held.tile([P, HALVES], F32, name="inv_total")
+        nc.vector.reciprocal(inv_total[:], total[:])
+        score = held.tile(per_slot, F32, name="score")
+        nc.vector.tensor_tensor(score[:], expd[:], inv_total[:].unsqueeze(2).to_broadcast(per_slot), ALU.mult)
+
+        outT = [held.tile([P, P], F32, name=f"outT{h}") for h in range(HALVES)]
+        for t in range(SLOTS):
+            for h in range(HALVES):
+                p, b = divmod(t * HALVES + h, BLOCKS)
+                weight = score[:, h, t : t + 1]
+                if t == 0:
+                    nc.vector.tensor_scalar(outT[h][:], kvT_ps[p][:, b, :], weight, None, op0=ALU.mult)
+                else:
+                    nc.vector.scalar_tensor_tensor(
+                        outT[h][:], kvT_ps[p][:, b, :], weight, outT[h][:], op0=ALU.mult, op1=ALU.add
+                    )
+
+        out_ps = small_banks.tile([P, B], F32, name="out_ps", tag="wide")
+        for h in range(HALVES):
+            nc.tensor.transpose(out_ps[:, h * P : (h + 1) * P], outT[h][:], ident[:])
+        out_sb = held.tile([P, B], F32, name="out_sb")
+        nc.vector.tensor_copy(out_sb[:], out_ps[:])
+        nc.sync.dma_start(out, out_sb[:])

@@ -56,7 +56,7 @@ def tile_memory_kernel(tc, table, w, query, sim_q, sim_k, sim_b, offs, out):
             piece_offsets = offsets[:, p * (PIECE // 16) : (p + 1) * (PIECE // 16)]
             nc.tensor.matmul(kv_ps[p][:], w_sb[:], table_sb[:].indirect(piece_offsets), start=True, stop=True)
 
-        q_ps = small_banks.tile([P, B], F32, name="q_ps", tag="wide")
+        q_ps = small_banks.tile([P, B], F32, name="q_ps")
         nc.tensor.matmul(q_ps[:], w_sb[:], query_sb[:], start=True, stop=True)
         q_bf = held.tile([P, B], BF16, name="q_bf")
         nc.vector.tensor_copy(q_bf[:], q_ps[:])
@@ -106,21 +106,21 @@ def tile_memory_kernel(tc, table, w, query, sim_q, sim_k, sim_b, offs, out):
         score = held.tile(per_slot, F32, name="score")
         nc.vector.tensor_tensor(score[:], expd[:], inv_total[:].unsqueeze(2).to_broadcast(per_slot), ALU.mult)
 
-        outT = [held.tile([P, P], F32, name=f"outT{h}") for h in range(HALVES)]
+        out_ps = [small_banks.tile([P, P], F32, name=f"out_ps{h}") for h in range(HALVES)]
         for t in range(SLOTS):
             for h in range(HALVES):
                 p, b = divmod(t * HALVES + h, BLOCKS)
                 weight = score[:, h, t : t + 1]
-                if t == 0:
-                    nc.vector.tensor_scalar(outT[h][:], kvT_ps[p][:, b, :], weight, None, op0=ALU.mult)
+                scaled = held.tile([P, P], F32, name=f"scaled{t}_{h}")
+                if h == 0:
+                    nc.vector.tensor_scalar(scaled[:], kvT_ps[p][:, b, :], weight, None, op0=ALU.mult)
                 else:
-                    nc.vector.scalar_tensor_tensor(
-                        outT[h][:], kvT_ps[p][:, b, :], weight, outT[h][:], op0=ALU.mult, op1=ALU.add
-                    )
+                    nc.scalar.activation(scaled[:], kvT_ps[p][:, b, :], FUNC.Copy, scale=weight)
+                nc.tensor.matmul(
+                    out_ps[h][:], scaled[:], ident[:], is_transpose=True, start=(t == 0), stop=(t == SLOTS - 1)
+                )
 
-        out_ps = small_banks.tile([P, B], F32, name="out_ps", tag="wide")
-        for h in range(HALVES):
-            nc.tensor.transpose(out_ps[:, h * P : (h + 1) * P], outT[h][:], ident[:])
         out_sb = held.tile([P, B], F32, name="out_sb")
-        nc.vector.tensor_copy(out_sb[:], out_ps[:])
+        nc.vector.tensor_copy(out_sb[:, 0:P], out_ps[0][:])
+        nc.scalar.activation(out_sb[:, P:B], out_ps[1][:], FUNC.Copy)
         nc.sync.dma_start(out, out_sb[:])

@@ -15,6 +15,8 @@ HALVES = B // P
 PIECE = 512
 PIECES = N // PIECE
 BLOCKS = PIECE // P
+PER_PIECE = PIECE // B
+WARMUPS = 5
 
 FLOPS = 2 * P * P * (N + B) + 2 * P * (N + B) + 2 * P * N
 
@@ -26,6 +28,14 @@ def tile_memory_kernel(tc, table, w, query, sim_q, sim_k, sim_b, offs, out):
         tc.psum_pool(name="kv_banks", bufs=PIECES) as kv_banks,
         tc.psum_pool(name="small_banks", bufs=1) as small_banks,
     ):
+        zeros = held.tile([P, 1], BF16, name="zeros")
+        nc.gpsimd.memset(zeros[:], 0.0)
+        idle_ps = small_banks.tile([P, PIECE], F32, name="idle_ps", tag="early")
+        for k in range(WARMUPS):
+            nc.tensor.matmul(
+                idle_ps[:], zeros[:].to_broadcast([P, P]), zeros[:].to_broadcast([P, PIECE]), start=True, stop=True
+            )
+
         offsets = held.tile([P, N // 16], U16, name="offsets")
         nc.sync.dma_start(offsets[:], offs)
         table_sb = held.tile([P, S], BF16, name="table_sb")
@@ -48,7 +58,7 @@ def tile_memory_kernel(tc, table, w, query, sim_q, sim_k, sim_b, offs, out):
         ident = held.tile([P, P], F32, name="ident")
         make_identity(nc, ident[:])
 
-        logit_ps = small_banks.tile([P, HALVES * SLOTS + HALVES], F32, name="logit_ps")
+        logit_ps = small_banks.tile([P, HALVES * SLOTS], F32, name="logit_ps")
 
         kv_ps = []
         for p in range(PIECES):
@@ -56,31 +66,41 @@ def tile_memory_kernel(tc, table, w, query, sim_q, sim_k, sim_b, offs, out):
             piece_offsets = offsets[:, p * (PIECE // 16) : (p + 1) * (PIECE // 16)]
             nc.tensor.matmul(kv_ps[p][:], w_sb[:], table_sb[:].indirect(piece_offsets), start=True, stop=True)
 
-        q_ps = small_banks.tile([P, B], F32, name="q_ps")
-        nc.tensor.matmul(q_ps[:], w_sb[:], query_sb[:], start=True, stop=True)
+        q_ps = small_banks.tile([P, B + HALVES], F32, name="q_ps", tag="early")
+        nc.tensor.matmul(q_ps[:, :B], w_sb[:], query_sb[:], start=True, stop=True)
         q_bf = held.tile([P, B], BF16, name="q_bf")
-        nc.vector.tensor_copy(q_bf[:], q_ps[:])
+        nc.vector.tensor_copy(q_bf[:], q_ps[:, :B])
         for h in range(HALVES):
-            col = HALVES * SLOTS + h
             nc.tensor.matmul(
-                logit_ps[:, col : col + 1], q_bf[:, h * P : (h + 1) * P], simq_sb[:], start=True, stop=True
+                q_ps[:, B + h : B + h + 1], q_bf[:, h * P : (h + 1) * P], simq_sb[:], start=True, stop=True
             )
         q_term = held.tile([P, HALVES], F32, name="q_term")
-        nc.vector.tensor_scalar(q_term[:], logit_ps[:, HALVES * SLOTS :], bias_sb[:, 0:1], None, op0=ALU.add)
+        nc.vector.tensor_scalar(q_term[:], q_ps[:, B:], bias_sb[:, 0:1], None, op0=ALU.add)
 
         kvT_ps = []
-        for p in range(PIECES):
+
+        def score_piece(p):
             kv_bf = held.tile([P, PIECE], BF16, name=f"kv_bf{p}")
             nc.scalar.activation(kv_bf[:], kv_ps[p][:], FUNC.Copy)
+            for b in range(BLOCKS):
+                t, h = divmod(p * BLOCKS + b, HALVES)
+                col = h * SLOTS + t
+                nc.tensor.matmul(
+                    logit_ps[:, col : col + 1], kv_bf[:, b * P : (b + 1) * P], simk_sb[:], start=True, stop=True
+                )
+
+        def flip_piece(p):
             kv_sb = held.tile([P, PIECE], F32, name=f"kv_sb{p}")
             nc.vector.tensor_copy(kv_sb[:], kv_ps[p][:])
             kvT_ps.append(kv_banks.tile([P, BLOCKS, P], F32, name=f"kvT_ps{p}", tag="bank"))
             for b in range(BLOCKS):
-                t, h = divmod(p * BLOCKS + b, HALVES)
-                col = h * SLOTS + t
-                block = slice(b * P, (b + 1) * P)
-                nc.tensor.matmul(logit_ps[:, col : col + 1], kv_bf[:, block], simk_sb[:], start=True, stop=True)
-                nc.tensor.transpose(kvT_ps[p][:, b, :], kv_sb[:, block], ident[:])
+                nc.tensor.transpose(kvT_ps[p][:, b, :], kv_sb[:, b * P : (b + 1) * P], ident[:])
+
+        for p in range(PIECES):
+            score_piece(p)
+            if p > 0:
+                flip_piece(p - 1)
+        flip_piece(PIECES - 1)
 
         logit = held.tile([P, HALVES, SLOTS], F32, name="logit")
         for h in range(HALVES):
@@ -93,34 +113,53 @@ def tile_memory_kernel(tc, table, w, query, sim_q, sim_k, sim_b, offs, out):
                 op1=ALU.max,
             )
         per_slot = [P, HALVES, SLOTS]
-        top = held.tile([P, HALVES], F32, name="top")
-        nc.vector.tensor_reduce(top[:], logit[:], axis=X, op=ALU.max)
-        shifted = held.tile(per_slot, F32, name="shifted")
-        nc.vector.tensor_tensor(shifted[:], logit[:], top[:].unsqueeze(2).to_broadcast(per_slot), ALU.subtract)
+        neg_top = held.tile([P, HALVES], F32, name="neg_top")
+        nc.vector.tensor_reduce(neg_top[:], logit[:], axis=X, op=ALU.max, negate=True)
         expd = held.tile(per_slot, F32, name="expd")
-        nc.scalar.activation(expd[:], shifted[:], FUNC.Exp)
         total = held.tile([P, HALVES], F32, name="total")
-        nc.vector.tensor_reduce(total[:], expd[:], axis=X, op=ALU.add)
+        for h in range(HALVES):
+            nc.scalar.activation(
+                expd[:, h, :], logit[:, h, :], FUNC.Exp, bias=neg_top[:, h : h + 1], accum_out=total[:, h : h + 1]
+            )
+
         inv_total = held.tile([P, HALVES], F32, name="inv_total")
         nc.vector.reciprocal(inv_total[:], total[:])
-        score = held.tile(per_slot, F32, name="score")
-        nc.vector.tensor_tensor(score[:], expd[:], inv_total[:].unsqueeze(2).to_broadcast(per_slot), ALU.mult)
+        inv_ps = small_banks.tile([P, B], F32, name="inv_ps", tag="early")
+        for h in range(HALVES):
+            nc.tensor.transpose(inv_ps[:, h * P : (h + 1) * P], inv_total[:, h : h + 1].to_broadcast([P, P]), ident[:])
 
         out_ps = [small_banks.tile([P, P], F32, name=f"out_ps{h}") for h in range(HALVES)]
-        for t in range(SLOTS):
-            for h in range(HALVES):
-                p, b = divmod(t * HALVES + h, BLOCKS)
-                weight = score[:, h, t : t + 1]
-                scaled = held.tile([P, P], F32, name=f"scaled{t}_{h}")
-                if h == 0:
-                    nc.vector.tensor_scalar(scaled[:], kvT_ps[p][:, b, :], weight, None, op0=ALU.mult)
-                else:
-                    nc.scalar.activation(scaled[:], kvT_ps[p][:, b, :], FUNC.Copy, scale=weight)
-                nc.tensor.matmul(
-                    out_ps[h][:], scaled[:], ident[:], is_transpose=True, start=(t == 0), stop=(t == SLOTS - 1)
-                )
+        for h in range(HALVES):
+            for p in range(0, PIECES, 2):
+                for u in range(PER_PIECE):
+                    b = u * HALVES + h
+                    t_even, t_odd = p * PER_PIECE + u, (p + 1) * PER_PIECE + u
+                    one = held.tile([P, P], F32, name=f"one{p}_{b}")
+                    nc.scalar.activation(
+                        one[:], kvT_ps[p][:, b, :], FUNC.Copy, scale=expd[:, h, t_even : t_even + 1]
+                    )
+                    two = held.tile([P, P], F32, name=f"two{p}_{b}")
+                    nc.vector.scalar_tensor_tensor(
+                        two[:],
+                        kvT_ps[p + 1][:, b, :],
+                        expd[:, h, t_odd : t_odd + 1],
+                        one[:],
+                        op0=ALU.mult,
+                        op1=ALU.add,
+                    )
+                    nc.tensor.matmul(
+                        out_ps[h][:],
+                        two[:],
+                        ident[:],
+                        is_transpose=True,
+                        start=(p == 0 and u == 0),
+                        stop=(p == PIECES - 2 and u == PER_PIECE - 1),
+                    )
 
+        inv_sb = held.tile([P, B], F32, name="inv_sb")
+        nc.scalar.activation(inv_sb[:], inv_ps[:], FUNC.Copy)
         out_sb = held.tile([P, B], F32, name="out_sb")
-        nc.vector.tensor_copy(out_sb[:, 0:P], out_ps[0][:])
-        nc.scalar.activation(out_sb[:, P:B], out_ps[1][:], FUNC.Copy)
-        nc.sync.dma_start(out, out_sb[:])
+        for h in range(HALVES):
+            half = slice(h * P, (h + 1) * P)
+            nc.vector.tensor_tensor(out_sb[:, half], out_ps[h][:], inv_sb[:, half], ALU.mult)
+            nc.sync.dma_start(out[:, half], out_sb[:, half])

@@ -16,7 +16,6 @@ PIECE = 512
 PIECES = N // PIECE
 BLOCKS = PIECE // P
 PER_PIECE = PIECE // B
-WARMUPS = 5
 
 FLOPS = 2 * P * P * (N + B) + 2 * P * (N + B) + 2 * P * N
 
@@ -28,14 +27,6 @@ def tile_memory_kernel(tc, table, w, query, sim_q, sim_k, sim_b, offs, out):
         tc.psum_pool(name="kv_banks", bufs=PIECES) as kv_banks,
         tc.psum_pool(name="small_banks", bufs=1) as small_banks,
     ):
-        zeros = held.tile([P, 1], BF16, name="zeros")
-        nc.gpsimd.memset(zeros[:], 0.0)
-        idle_ps = small_banks.tile([P, PIECE], F32, name="idle_ps", tag="early")
-        for k in range(WARMUPS):
-            nc.tensor.matmul(
-                idle_ps[:], zeros[:].to_broadcast([P, P]), zeros[:].to_broadcast([P, PIECE]), start=True, stop=True
-            )
-
         offsets = held.tile([P, N // 16], U16, name="offsets")
         nc.sync.dma_start(offsets[:], offs)
         table_sb = held.tile([P, S], BF16, name="table_sb")

@@ -49,7 +49,11 @@ def tile_memory_kernel(tc, table, w, query, sim_q, sim_k, sim_b, offs, out):
         ident = held.tile([P, P], F32, name="ident")
         make_identity(nc, ident[:])
 
-        logit_ps = small_banks.tile([P, HALVES * SLOTS], F32, name="logit_ps")
+        def copy_from_bank(p, dst, src):
+            if p % 2 == 1:
+                nc.scalar.activation(dst, src, FUNC.Copy)
+            else:
+                nc.vector.tensor_copy(dst, src)
 
         kv_ps = []
         for p in range(PIECES):
@@ -57,7 +61,7 @@ def tile_memory_kernel(tc, table, w, query, sim_q, sim_k, sim_b, offs, out):
             piece_offsets = offsets[:, p * (PIECE // 16) : (p + 1) * (PIECE // 16)]
             nc.tensor.matmul(kv_ps[p][:], w_sb[:], table_sb[:].indirect(piece_offsets), start=True, stop=True)
 
-        q_ps = small_banks.tile([P, B + HALVES], F32, name="q_ps", tag="early")
+        q_ps = small_banks.tile([P, B + HALVES], F32, name="q_ps", tag="q_then_inv")
         nc.tensor.matmul(q_ps[:, :B], w_sb[:], query_sb[:], start=True, stop=True)
         q_bf = held.tile([P, B], BF16, name="q_bf")
         nc.vector.tensor_copy(q_bf[:], q_ps[:, :B])
@@ -68,11 +72,12 @@ def tile_memory_kernel(tc, table, w, query, sim_q, sim_k, sim_b, offs, out):
         q_term = held.tile([P, HALVES], F32, name="q_term")
         nc.vector.tensor_scalar(q_term[:], q_ps[:, B:], bias_sb[:, 0:1], None, op0=ALU.add)
 
+        logit_ps = small_banks.tile([P, HALVES * SLOTS], F32, name="logit_ps")
         kvT_ps = []
 
         def score_piece(p):
             kv_bf = held.tile([P, PIECE], BF16, name=f"kv_bf{p}")
-            nc.scalar.activation(kv_bf[:], kv_ps[p][:], FUNC.Copy)
+            copy_from_bank(p, kv_bf[:], kv_ps[p][:])
             for b in range(BLOCKS):
                 t, h = divmod(p * BLOCKS + b, HALVES)
                 col = h * SLOTS + t
@@ -82,7 +87,7 @@ def tile_memory_kernel(tc, table, w, query, sim_q, sim_k, sim_b, offs, out):
 
         def flip_piece(p):
             kv_sb = held.tile([P, PIECE], F32, name=f"kv_sb{p}")
-            nc.vector.tensor_copy(kv_sb[:], kv_ps[p][:])
+            copy_from_bank(p, kv_sb[:], kv_ps[p][:])
             kvT_ps.append(kv_banks.tile([P, BLOCKS, P], F32, name=f"kvT_ps{p}", tag="bank"))
             for b in range(BLOCKS):
                 nc.tensor.transpose(kvT_ps[p][:, b, :], kv_sb[:, b * P : (b + 1) * P], ident[:])
@@ -103,10 +108,9 @@ def tile_memory_kernel(tc, table, w, query, sim_q, sim_k, sim_b, offs, out):
                 op0=ALU.add,
                 op1=ALU.max,
             )
-        per_slot = [P, HALVES, SLOTS]
         neg_top = held.tile([P, HALVES], F32, name="neg_top")
         nc.vector.tensor_reduce(neg_top[:], logit[:], axis=X, op=ALU.max, negate=True)
-        expd = held.tile(per_slot, F32, name="expd")
+        expd = held.tile([P, HALVES, SLOTS], F32, name="expd")
         total = held.tile([P, HALVES], F32, name="total")
         for h in range(HALVES):
             nc.scalar.activation(
@@ -115,7 +119,7 @@ def tile_memory_kernel(tc, table, w, query, sim_q, sim_k, sim_b, offs, out):
 
         inv_total = held.tile([P, HALVES], F32, name="inv_total")
         nc.vector.reciprocal(inv_total[:], total[:])
-        inv_ps = small_banks.tile([P, B], F32, name="inv_ps", tag="early")
+        inv_ps = small_banks.tile([P, B], F32, name="inv_ps", tag="q_then_inv")
         for h in range(HALVES):
             nc.tensor.transpose(inv_ps[:, h * P : (h + 1) * P], inv_total[:, h : h + 1].to_broadcast([P, P]), ident[:])
 
@@ -125,22 +129,22 @@ def tile_memory_kernel(tc, table, w, query, sim_q, sim_k, sim_b, offs, out):
                 for u in range(PER_PIECE):
                     b = u * HALVES + h
                     t_even, t_odd = p * PER_PIECE + u, (p + 1) * PER_PIECE + u
-                    one = held.tile([P, P], F32, name=f"one{p}_{b}")
+                    odd_part = held.tile([P, P], F32, name=f"odd_part{p}_{b}")
                     nc.scalar.activation(
-                        one[:], kvT_ps[p][:, b, :], FUNC.Copy, scale=expd[:, h, t_even : t_even + 1]
+                        odd_part[:], kvT_ps[p + 1][:, b, :], FUNC.Copy, scale=expd[:, h, t_odd : t_odd + 1]
                     )
-                    two = held.tile([P, P], F32, name=f"two{p}_{b}")
+                    pair_sum = held.tile([P, P], F32, name=f"pair_sum{p}_{b}")
                     nc.vector.scalar_tensor_tensor(
-                        two[:],
-                        kvT_ps[p + 1][:, b, :],
-                        expd[:, h, t_odd : t_odd + 1],
-                        one[:],
+                        pair_sum[:],
+                        kvT_ps[p][:, b, :],
+                        expd[:, h, t_even : t_even + 1],
+                        odd_part[:],
                         op0=ALU.mult,
                         op1=ALU.add,
                     )
                     nc.tensor.matmul(
                         out_ps[h][:],
-                        two[:],
+                        pair_sum[:],
                         ident[:],
                         is_transpose=True,
                         start=(p == 0 and u == 0),

@@ -27,14 +27,14 @@ def tile_memory_kernel(tc, table, w, query, sim_q, sim_k, sim_b, offs, out):
         tc.psum_pool(name="kv_banks", bufs=PIECES) as kv_banks,
         tc.psum_pool(name="small_banks", bufs=1) as small_banks,
     ):
-        offsets = held.tile([P, N // 16], U16, name="offsets")
-        nc.sync.dma_start(offsets[:], offs)
         table_sb = held.tile([P, S], BF16, name="table_sb")
         nc.scalar.dma_start(table_sb[:], table)
         w_sb = held.tile([P, P], BF16, name="w_sb")
         nc.sync.dma_start(w_sb[:], w)
         query_sb = held.tile([P, B], BF16, name="query_sb")
         nc.sync.dma_start(query_sb[:], query)
+        offsets = held.tile([P, N // 16], U16, name="offsets")
+        nc.sync.dma_start(offsets[:], offs)
         simk_sb = held.tile([P, 1], BF16, name="simk_sb")
         nc.scalar.dma_start(simk_sb[:], sim_k)
         simq_sb = held.tile([P, 1], BF16, name="simq_sb")
@@ -55,16 +55,17 @@ def tile_memory_kernel(tc, table, w, query, sim_q, sim_k, sim_b, offs, out):
             else:
                 nc.vector.tensor_copy(dst, src)
 
+        q_ps = small_banks.tile([P, B + HALVES], F32, name="q_ps", tag="q_then_inv")
+        nc.tensor.matmul(q_ps[:, :B], w_sb[:], query_sb[:], start=True, stop=True)
+        q_bf = held.tile([P, B], BF16, name="q_bf")
+        nc.vector.tensor_copy(q_bf[:], q_ps[:, :B])
+
         kv_ps = []
         for p in range(PIECES):
             kv_ps.append(kv_banks.tile([P, PIECE], F32, name=f"kv_ps{p}", tag="bank"))
             piece_offsets = offsets[:, p * (PIECE // 16) : (p + 1) * (PIECE // 16)]
             nc.tensor.matmul(kv_ps[p][:], w_sb[:], table_sb[:].indirect(piece_offsets), start=True, stop=True)
 
-        q_ps = small_banks.tile([P, B + HALVES], F32, name="q_ps", tag="q_then_inv")
-        nc.tensor.matmul(q_ps[:, :B], w_sb[:], query_sb[:], start=True, stop=True)
-        q_bf = held.tile([P, B], BF16, name="q_bf")
-        nc.vector.tensor_copy(q_bf[:], q_ps[:, :B])
         for h in range(HALVES):
             nc.tensor.matmul(
                 q_ps[:, B + h : B + h + 1], q_bf[:, h * P : (h + 1) * P], simq_sb[:], start=True, stop=True
@@ -124,32 +125,31 @@ def tile_memory_kernel(tc, table, w, query, sim_q, sim_k, sim_b, offs, out):
             nc.tensor.transpose(inv_ps[:, h * P : (h + 1) * P], inv_total[:, h : h + 1].to_broadcast([P, P]), ident[:])
 
         out_ps = [small_banks.tile([P, P], F32, name=f"out_ps{h}") for h in range(HALVES)]
-        for h in range(HALVES):
-            for p in range(0, PIECES, 2):
-                for u in range(PER_PIECE):
-                    b = u * HALVES + h
-                    t_even, t_odd = p * PER_PIECE + u, (p + 1) * PER_PIECE + u
-                    odd_part = held.tile([P, P], F32, name=f"odd_part{p}_{b}")
-                    nc.scalar.activation(
-                        odd_part[:], kvT_ps[p + 1][:, b, :], FUNC.Copy, scale=expd[:, h, t_odd : t_odd + 1]
-                    )
-                    pair_sum = held.tile([P, P], F32, name=f"pair_sum{p}_{b}")
-                    nc.vector.scalar_tensor_tensor(
-                        pair_sum[:],
-                        kvT_ps[p][:, b, :],
-                        expd[:, h, t_even : t_even + 1],
-                        odd_part[:],
-                        op0=ALU.mult,
-                        op1=ALU.add,
-                    )
-                    nc.tensor.matmul(
-                        out_ps[h][:],
-                        pair_sum[:],
-                        ident[:],
-                        is_transpose=True,
-                        start=(p == 0 and u == 0),
-                        stop=(p == PIECES - 2 and u == PER_PIECE - 1),
-                    )
+        for p in range(0, PIECES, 2):
+            for b in range(BLOCKS):
+                u, h = divmod(b, HALVES)
+                t_even, t_odd = p * PER_PIECE + u, (p + 1) * PER_PIECE + u
+                odd_part = held.tile([P, P], F32, name=f"odd_part{p}_{b}")
+                nc.scalar.activation(
+                    odd_part[:], kvT_ps[p + 1][:, b, :], FUNC.Copy, scale=expd[:, h, t_odd : t_odd + 1]
+                )
+                pair_sum = held.tile([P, P], F32, name=f"pair_sum{p}_{b}")
+                nc.vector.scalar_tensor_tensor(
+                    pair_sum[:],
+                    kvT_ps[p][:, b, :],
+                    expd[:, h, t_even : t_even + 1],
+                    odd_part[:],
+                    op0=ALU.mult,
+                    op1=ALU.add,
+                )
+                nc.tensor.matmul(
+                    out_ps[h][:],
+                    pair_sum[:],
+                    ident[:],
+                    is_transpose=True,
+                    start=(p == 0 and u == 0),
+                    stop=(p == PIECES - 2 and u == PER_PIECE - 1),
+                )
 
         inv_sb = held.tile([P, B], F32, name="inv_sb")
         nc.scalar.activation(inv_sb[:], inv_ps[:], FUNC.Copy)

@@ -27,14 +27,14 @@ def tile_memory_kernel(tc, table, w, query, sim_q, sim_k, sim_b, offs, out):
         tc.psum_pool(name="kv_banks", bufs=PIECES) as kv_banks,
         tc.psum_pool(name="small_banks", bufs=1) as small_banks,
     ):
+        offsets = held.tile([P, N // 16], U16, name="offsets")
+        nc.sync.dma_start(offsets[:], offs)
         table_sb = held.tile([P, S], BF16, name="table_sb")
         nc.scalar.dma_start(table_sb[:], table)
         w_sb = held.tile([P, P], BF16, name="w_sb")
         nc.sync.dma_start(w_sb[:], w)
         query_sb = held.tile([P, B], BF16, name="query_sb")
         nc.sync.dma_start(query_sb[:], query)
-        offsets = held.tile([P, N // 16], U16, name="offsets")
-        nc.sync.dma_start(offsets[:], offs)
         simk_sb = held.tile([P, 1], BF16, name="simk_sb")
         nc.scalar.dma_start(simk_sb[:], sim_k)
         simq_sb = held.tile([P, 1], BF16, name="simq_sb")
@@ -55,17 +55,16 @@ def tile_memory_kernel(tc, table, w, query, sim_q, sim_k, sim_b, offs, out):
             else:
                 nc.vector.tensor_copy(dst, src)
 
-        q_ps = small_banks.tile([P, B + HALVES], F32, name="q_ps", tag="q_then_inv")
-        nc.tensor.matmul(q_ps[:, :B], w_sb[:], query_sb[:], start=True, stop=True)
-        q_bf = held.tile([P, B], BF16, name="q_bf")
-        nc.vector.tensor_copy(q_bf[:], q_ps[:, :B])
-
         kv_ps = []
         for p in range(PIECES):
             kv_ps.append(kv_banks.tile([P, PIECE], F32, name=f"kv_ps{p}", tag="bank"))
             piece_offsets = offsets[:, p * (PIECE // 16) : (p + 1) * (PIECE // 16)]
             nc.tensor.matmul(kv_ps[p][:], w_sb[:], table_sb[:].indirect(piece_offsets), start=True, stop=True)
 
+        q_ps = small_banks.tile([P, B + HALVES], F32, name="q_ps", tag="q_then_inv")
+        nc.tensor.matmul(q_ps[:, :B], w_sb[:], query_sb[:], start=True, stop=True)
+        q_bf = held.tile([P, B], BF16, name="q_bf")
+        nc.vector.tensor_copy(q_bf[:], q_ps[:, :B])
         for h in range(HALVES):
             nc.tensor.matmul(
                 q_ps[:, B + h : B + h + 1], q_bf[:, h * P : (h + 1) * P], simq_sb[:], start=True, stop=True
@@ -125,31 +124,32 @@ def tile_memory_kernel(tc, table, w, query, sim_q, sim_k, sim_b, offs, out):
             nc.tensor.transpose(inv_ps[:, h * P : (h + 1) * P], inv_total[:, h : h + 1].to_broadcast([P, P]), ident[:])
 
         out_ps = [small_banks.tile([P, P], F32, name=f"out_ps{h}") for h in range(HALVES)]
-        for p in range(0, PIECES, 2):
-            for b in range(BLOCKS):
-                u, h = divmod(b, HALVES)
-                t_even, t_odd = p * PER_PIECE + u, (p + 1) * PER_PIECE + u
-                odd_part = held.tile([P, P], F32, name=f"odd_part{p}_{b}")
-                nc.scalar.activation(
-                    odd_part[:], kvT_ps[p + 1][:, b, :], FUNC.Copy, scale=expd[:, h, t_odd : t_odd + 1]
-                )
-                pair_sum = held.tile([P, P], F32, name=f"pair_sum{p}_{b}")
-                nc.vector.scalar_tensor_tensor(
-                    pair_sum[:],
-                    kvT_ps[p][:, b, :],
-                    expd[:, h, t_even : t_even + 1],
-                    odd_part[:],
-                    op0=ALU.mult,
-                    op1=ALU.add,
-                )
-                nc.tensor.matmul(
-                    out_ps[h][:],
-                    pair_sum[:],
-                    ident[:],
-                    is_transpose=True,
-                    start=(p == 0 and u == 0),
-                    stop=(p == PIECES - 2 and u == PER_PIECE - 1),
-                )
+        for h in range(HALVES):
+            for p in range(0, PIECES, 2):
+                for u in range(PER_PIECE):
+                    b = u * HALVES + h
+                    t_even, t_odd = p * PER_PIECE + u, (p + 1) * PER_PIECE + u
+                    even_part = held.tile([P, P], F32, name=f"even_part{p}_{b}")
+                    nc.scalar.activation(
+                        even_part[:], kvT_ps[p][:, b, :], FUNC.Copy, scale=expd[:, h, t_even : t_even + 1]
+                    )
+                    pair_sum = held.tile([P, P], F32, name=f"pair_sum{p}_{b}")
+                    nc.vector.scalar_tensor_tensor(
+                        pair_sum[:],
+                        kvT_ps[p + 1][:, b, :],
+                        expd[:, h, t_odd : t_odd + 1],
+                        even_part[:],
+                        op0=ALU.mult,
+                        op1=ALU.add,
+                    )
+                    nc.tensor.matmul(
+                        out_ps[h][:],
+                        pair_sum[:],
+                        ident[:],
+                        is_transpose=True,
+                        start=(p == 0 and u == 0),
+                        stop=(p == PIECES - 2 and u == PER_PIECE - 1),
+                    )
 
         inv_sb = held.tile([P, B], F32, name="inv_sb")
         nc.scalar.activation(inv_sb[:], inv_ps[:], FUNC.Copy)

@@ -12,10 +12,13 @@ SLOTS = 8
 B = 256
 N = SLOTS * B
 HALVES = B // P
-PIECE = 512
-PIECES = N // PIECE
-BLOCKS = PIECE // P
-PER_PIECE = PIECE // B
+BANK_BLOCKS = 4
+GROUPS = N // (BANK_BLOCKS * P)
+PER_GROUP = BANK_BLOCKS // HALVES
+PIECE_BLOCKS = (4, 4, 4, 2, 1, 1)
+PIECES = len(PIECE_BLOCKS)
+FIRST_BLOCK = tuple(sum(PIECE_BLOCKS[:k]) for k in range(PIECES))
+PSUM_BANKS = 8
 
 FLOPS = 2 * P * P * (N + B) + 2 * P * (N + B) + 2 * P * N
 
@@ -24,8 +27,8 @@ def tile_memory_kernel(tc, table, w, query, sim_q, sim_k, sim_b, offs, out):
     nc = tc.nc
     with (
         tc.tile_pool(name="held", bufs=1) as held,
-        tc.psum_pool(name="kv_banks", bufs=PIECES) as kv_banks,
-        tc.psum_pool(name="small_banks", bufs=1) as small_banks,
+        tc.psum_pool(name="logit_bank", bufs=1) as logit_bank,
+        tc.psum_pool(name="banks", bufs=PSUM_BANKS - 1) as banks,
     ):
         offsets = held.tile([P, N // 16], U16, name="offsets")
         nc.sync.dma_start(offsets[:], offs)
@@ -41,6 +44,8 @@ def tile_memory_kernel(tc, table, w, query, sim_q, sim_k, sim_b, offs, out):
         nc.scalar.dma_start(simq_sb[:], sim_q)
         bias_sb = held.tile([P, 1], F32, name="bias_sb")
         nc.sync.dma_start(bias_sb[:], sim_b.partition_broadcast(P))
+        neg_bias = held.tile([P, 1], F32, name="neg_bias")
+        nc.vector.tensor_scalar(neg_bias[:], bias_sb[:], -1.0, None, op0=ALU.mult)
 
         warm = held.tile([P, 1], F32, name="warm")
         nc.vector.memset(warm[:], 0.0)
@@ -57,54 +62,50 @@ def tile_memory_kernel(tc, table, w, query, sim_q, sim_k, sim_b, offs, out):
 
         kv_ps = []
         for p in range(PIECES):
-            kv_ps.append(kv_banks.tile([P, PIECE], F32, name=f"kv_ps{p}", tag="bank"))
-            piece_offsets = offsets[:, p * (PIECE // 16) : (p + 1) * (PIECE // 16)]
+            kv_ps.append(banks.tile([P, PIECE_BLOCKS[p] * P], F32, name=f"kv_ps{p}", tag="bank"))
+            first_col = FIRST_BLOCK[p] * P // 16
+            piece_offsets = offsets[:, first_col : first_col + PIECE_BLOCKS[p] * P // 16]
             nc.tensor.matmul(kv_ps[p][:], w_sb[:], table_sb[:].indirect(piece_offsets), start=True, stop=True)
 
-        q_ps = small_banks.tile([P, B + HALVES], F32, name="q_ps", tag="q_then_inv")
+        q_ps = banks.tile([P, B + HALVES], F32, name="q_ps", tag="bank")
         nc.tensor.matmul(q_ps[:, :B], w_sb[:], query_sb[:], start=True, stop=True)
+
+
+        logit_ps = logit_bank.tile([P, HALVES * SLOTS], F32, name="logit_ps")
+        for p in range(PIECES):
+            kv_bf = held.tile([P, PIECE_BLOCKS[p] * P], BF16, name=f"kv_bf{p}")
+            copy_from_bank(p, kv_bf[:], kv_ps[p][:])
+            for b in range(PIECE_BLOCKS[p]):
+                t, h = divmod(FIRST_BLOCK[p] + b, HALVES)
+                col = h * SLOTS + t
+                nc.tensor.matmul(
+                    logit_ps[:, col : col + 1], kv_bf[:, b * P : (b + 1) * P], simk_sb[:], start=True, stop=True
+                )
+
         q_bf = held.tile([P, B], BF16, name="q_bf")
         nc.vector.tensor_copy(q_bf[:], q_ps[:, :B])
         for h in range(HALVES):
             nc.tensor.matmul(
                 q_ps[:, B + h : B + h + 1], q_bf[:, h * P : (h + 1) * P], simq_sb[:], start=True, stop=True
             )
-        q_term = held.tile([P, HALVES], F32, name="q_term")
-        nc.vector.tensor_scalar(q_term[:], q_ps[:, B:], bias_sb[:, 0:1], None, op0=ALU.add)
 
-        logit_ps = small_banks.tile([P, HALVES * SLOTS], F32, name="logit_ps")
         kvT_ps = []
-
-        def score_piece(p):
-            kv_bf = held.tile([P, PIECE], BF16, name=f"kv_bf{p}")
-            copy_from_bank(p, kv_bf[:], kv_ps[p][:])
-            for b in range(BLOCKS):
-                t, h = divmod(p * BLOCKS + b, HALVES)
-                col = h * SLOTS + t
-                nc.tensor.matmul(
-                    logit_ps[:, col : col + 1], kv_bf[:, b * P : (b + 1) * P], simk_sb[:], start=True, stop=True
-                )
-
-        def flip_piece(p):
-            kv_sb = held.tile([P, PIECE], F32, name=f"kv_sb{p}")
-            copy_from_bank(p, kv_sb[:], kv_ps[p][:])
-            kvT_ps.append(kv_banks.tile([P, BLOCKS, P], F32, name=f"kvT_ps{p}", tag="bank"))
-            for b in range(BLOCKS):
-                nc.tensor.transpose(kvT_ps[p][:, b, :], kv_sb[:, b * P : (b + 1) * P], ident[:])
-
         for p in range(PIECES):
-            score_piece(p)
-            if p > 0:
-                flip_piece(p - 1)
-        flip_piece(PIECES - 1)
+            for b in range(PIECE_BLOCKS[p]):
+                g, place = divmod(FIRST_BLOCK[p] + b, BANK_BLOCKS)
+                if place == 0:
+                    kvT_ps.append(banks.tile([P, BANK_BLOCKS, P], F32, name=f"kvT_ps{g}", tag="bank"))
+                kv_sb = held.tile([P, P], F32, name=f"kv_sb{p}_{b}")
+                copy_from_bank(p, kv_sb[:], kv_ps[p][:, b * P : (b + 1) * P])
+                nc.tensor.transpose(kvT_ps[g][:, place, :], kv_sb[:], ident[:])
 
         logit = held.tile([P, HALVES, SLOTS], F32, name="logit")
         for h in range(HALVES):
             nc.vector.tensor_scalar(
                 logit[:, h, :],
                 logit_ps[:, h * SLOTS : (h + 1) * SLOTS],
-                q_term[:, h : h + 1],
-                0.0,
+                q_ps[:, B + h : B + h + 1],
+                neg_bias[:, 0:1],
                 op0=ALU.add,
                 op1=ALU.max,
             )
@@ -119,16 +120,16 @@ def tile_memory_kernel(tc, table, w, query, sim_q, sim_k, sim_b, offs, out):
 
         inv_total = held.tile([P, HALVES], F32, name="inv_total")
         nc.vector.reciprocal(inv_total[:], total[:])
-        inv_ps = small_banks.tile([P, B], F32, name="inv_ps", tag="q_then_inv")
+        inv_ps = banks.tile([P, B], F32, name="inv_ps", tag="bank")
         for h in range(HALVES):
             nc.tensor.transpose(inv_ps[:, h * P : (h + 1) * P], inv_total[:, h : h + 1].to_broadcast([P, P]), ident[:])
 
-        out_ps = [small_banks.tile([P, P], F32, name=f"out_ps{h}") for h in range(HALVES)]
+        out_ps = [banks.tile([P, P], F32, name=f"out_ps{h}", tag="bank") for h in range(HALVES)]
         for h in range(HALVES):
-            for p in range(0, PIECES, 2):
-                for u in range(PER_PIECE):
+            for p in range(0, GROUPS, 2):
+                for u in range(PER_GROUP):
                     b = u * HALVES + h
-                    t_even, t_odd = p * PER_PIECE + u, (p + 1) * PER_PIECE + u
+                    t_even, t_odd = p * PER_GROUP + u, (p + 1) * PER_GROUP + u
                     even_part = held.tile([P, P], F32, name=f"even_part{p}_{b}")
                     nc.scalar.activation(
                         even_part[:], kvT_ps[p][:, b, :], FUNC.Copy, scale=expd[:, h, t_even : t_even + 1]
@@ -148,7 +149,7 @@ def tile_memory_kernel(tc, table, w, query, sim_q, sim_k, sim_b, offs, out):
                         ident[:],
                         is_transpose=True,
                         start=(p == 0 and u == 0),
-                        stop=(p == PIECES - 2 and u == PER_PIECE - 1),
+                        stop=(p == GROUPS - 2 and u == PER_GROUP - 1),
                     )
 
         inv_sb = held.tile([P, B], F32, name="inv_sb")

@@ -44,8 +44,10 @@ def tile_memory_kernel(tc, table, w, query, sim_q, sim_k, sim_b, offs, out):
         nc.scalar.dma_start(simq_sb[:], sim_q)
         bias_sb = held.tile([P, 1], F32, name="bias_sb")
         nc.sync.dma_start(bias_sb[:], sim_b.partition_broadcast(P))
-        neg_bias = held.tile([P, 1], F32, name="neg_bias")
-        nc.vector.tensor_scalar(neg_bias[:], bias_sb[:], -1.0, None, op0=ALU.mult)
+        neg_simk = held.tile([P, 1], BF16, name="neg_simk")
+        nc.vector.tensor_scalar(neg_simk[:], simk_sb[:], -1.0, None, op0=ALU.mult)
+        neg_simq = held.tile([P, SLOTS], BF16, name="neg_simq")
+        nc.vector.tensor_scalar(neg_simq[:], simq_sb[:, 0:1].to_broadcast([P, SLOTS]), -1.0, None, op0=ALU.mult)
 
         warm = held.tile([P, 1], F32, name="warm")
         nc.vector.memset(warm[:], 0.0)
@@ -67,8 +69,8 @@ def tile_memory_kernel(tc, table, w, query, sim_q, sim_k, sim_b, offs, out):
             piece_offsets = offsets[:, first_col : first_col + PIECE_BLOCKS[p] * P // 16]
             nc.tensor.matmul(kv_ps[p][:], w_sb[:], table_sb[:].indirect(piece_offsets), start=True, stop=True)
 
-        q_ps = banks.tile([P, B + HALVES], F32, name="q_ps", tag="bank")
-        nc.tensor.matmul(q_ps[:, :B], w_sb[:], query_sb[:], start=True, stop=True)
+        q_ps = banks.tile([P, B], F32, name="q_ps", tag="bank")
+        nc.tensor.matmul(q_ps[:], w_sb[:], query_sb[:], start=True, stop=True)
 
 
         logit_ps = logit_bank.tile([P, HALVES * SLOTS], F32, name="logit_ps")
@@ -79,14 +81,22 @@ def tile_memory_kernel(tc, table, w, query, sim_q, sim_k, sim_b, offs, out):
                 t, h = divmod(FIRST_BLOCK[p] + b, HALVES)
                 col = h * SLOTS + t
                 nc.tensor.matmul(
-                    logit_ps[:, col : col + 1], kv_bf[:, b * P : (b + 1) * P], simk_sb[:], start=True, stop=True
+                    logit_ps[:, col : col + 1],
+                    kv_bf[:, b * P : (b + 1) * P],
+                    neg_simk[:],
+                    start=(p == 0 and b == 0),
+                    stop=False,
                 )
 
         q_bf = held.tile([P, B], BF16, name="q_bf")
-        nc.vector.tensor_copy(q_bf[:], q_ps[:, :B])
+        nc.vector.tensor_copy(q_bf[:], q_ps[:])
         for h in range(HALVES):
             nc.tensor.matmul(
-                q_ps[:, B + h : B + h + 1], q_bf[:, h * P : (h + 1) * P], simq_sb[:], start=True, stop=True
+                logit_ps[:, h * SLOTS : (h + 1) * SLOTS],
+                q_bf[:, h * P : (h + 1) * P],
+                neg_simq[:],
+                start=False,
+                stop=(h == HALVES - 1),
             )
 
         kvT_ps = []
@@ -99,23 +109,28 @@ def tile_memory_kernel(tc, table, w, query, sim_q, sim_k, sim_b, offs, out):
                 copy_from_bank(p, kv_sb[:], kv_ps[p][:, b * P : (b + 1) * P])
                 nc.tensor.transpose(kvT_ps[g][:, place, :], kv_sb[:], ident[:])
 
-        logit = held.tile([P, HALVES, SLOTS], F32, name="logit")
-        for h in range(HALVES):
-            nc.vector.tensor_scalar(
-                logit[:, h, :],
-                logit_ps[:, h * SLOTS : (h + 1) * SLOTS],
-                q_ps[:, B + h : B + h + 1],
-                neg_bias[:, 0:1],
-                op0=ALU.add,
-                op1=ALU.max,
-            )
+        neg_logit = held.tile([P, HALVES, SLOTS], F32, name="neg_logit")
         neg_top = held.tile([P, HALVES], F32, name="neg_top")
-        nc.vector.tensor_reduce(neg_top[:], logit[:], axis=X, op=ALU.max, negate=True)
         expd = held.tile([P, HALVES, SLOTS], F32, name="expd")
         total = held.tile([P, HALVES], F32, name="total")
         for h in range(HALVES):
+            nc.vector.tensor_scalar(
+                neg_logit[:, h, :],
+                logit_ps[:, h * SLOTS : (h + 1) * SLOTS],
+                bias_sb[:, 0:1],
+                None,
+                op0=ALU.min,
+                op1=ALU.min,
+                accum_out=neg_top[:, h : h + 1],
+            )
+        for h in range(HALVES):
             nc.scalar.activation(
-                expd[:, h, :], logit[:, h, :], FUNC.Exp, bias=neg_top[:, h : h + 1], accum_out=total[:, h : h + 1]
+                expd[:, h, :],
+                neg_logit[:, h, :],
+                FUNC.Exp,
+                bias=neg_top[:, h : h + 1],
+                scale=-1.0,
+                accum_out=total[:, h : h + 1],
             )
 
         inv_total = held.tile([P, HALVES], F32, name="inv_total")

@@ -69,7 +69,7 @@ def tile_memory_kernel(tc, table, w, query, sim_q, sim_k, sim_b, offs, out):
             piece_offsets = offsets[:, first_col : first_col + PIECE_BLOCKS[p] * P // 16]
             nc.tensor.matmul(kv_ps[p][:], w_sb[:], table_sb[:].indirect(piece_offsets), start=True, stop=True)
 
-        q_ps = banks.tile([P, B], F32, name="q_ps", tag="bank")
+        q_ps = banks.tile([P, B], BF16, name="q_ps", tag="bank")
         nc.tensor.matmul(q_ps[:], w_sb[:], query_sb[:], start=True, stop=True)
 
 

@@ -36,8 +36,6 @@ def tile_memory_kernel(tc, table, w, query, sim_q, sim_k, sim_b, offs, out):
         nc.scalar.dma_start(table_sb[:], table)
         w_sb = held.tile([P, P], BF16, name="w_sb")
         nc.sync.dma_start(w_sb[:], w)
-        query_sb = held.tile([P, B], BF16, name="query_sb")
-        nc.sync.dma_start(query_sb[:], query)
         simk_sb = held.tile([P, 1], BF16, name="simk_sb")
         nc.scalar.dma_start(simk_sb[:], sim_k)
         simq_sb = held.tile([P, 1], BF16, name="simq_sb")
@@ -55,6 +53,9 @@ def tile_memory_kernel(tc, table, w, query, sim_q, sim_k, sim_b, offs, out):
 
         ident = held.tile([P, P], F32, name="ident")
         make_identity(nc, ident[:])
+
+        query_sb = held.tile([P, B], BF16, name="query_sb")
+        nc.gpsimd.dma_start(query_sb[:], query)
 
         def copy_from_bank(p, dst, src):
             if p % 2 == 1:

@@ -131,8 +131,8 @@ def tile_memory_kernel(tc, table, w, query, sim_q, sim_k, sim_b, offs, out):
                 FUNC.Exp,
                 bias=neg_top[:, h : h + 1],
                 scale=-1.0,
-                accum_out=total[:, h : h + 1],
             )
+        nc.vector.tensor_reduce(total[:], expd[:], axis=X, op=ALU.add)
 
         inv_total = held.tile([P, HALVES], F32, name="inv_total")
         nc.vector.reciprocal(inv_total[:], total[:])

@@ -40,8 +40,6 @@ def tile_memory_kernel(tc, table, w, query, sim_q, sim_k, sim_b, offs, out):
         nc.scalar.dma_start(simk_sb[:], sim_k)
         simq_sb = held.tile([P, 1], BF16, name="simq_sb")
         nc.scalar.dma_start(simq_sb[:], sim_q)
-        bias_sb = held.tile([P, 1], F32, name="bias_sb")
-        nc.sync.dma_start(bias_sb[:], sim_b.partition_broadcast(P))
         neg_simk = held.tile([P, 1], BF16, name="neg_simk")
         nc.vector.tensor_scalar(neg_simk[:], simk_sb[:], -1.0, None, op0=ALU.mult)
         neg_simq = held.tile([P, SLOTS], BF16, name="neg_simq")
@@ -56,6 +54,8 @@ def tile_memory_kernel(tc, table, w, query, sim_q, sim_k, sim_b, offs, out):
 
         query_sb = held.tile([P, B], BF16, name="query_sb")
         nc.gpsimd.dma_start(query_sb[:], query)
+        bias_sb = held.tile([P, 1], F32, name="bias_sb")
+        nc.gpsimd.dma_start(bias_sb[:], sim_b.partition_broadcast(P))
 
         def copy_from_bank(p, dst, src):
             if p % 2 == 1:

@@ -40,10 +40,6 @@ def tile_memory_kernel(tc, table, w, query, sim_q, sim_k, sim_b, offs, out):
         nc.scalar.dma_start(simk_sb[:], sim_k)
         simq_sb = held.tile([P, 1], BF16, name="simq_sb")
         nc.scalar.dma_start(simq_sb[:], sim_q)
-        neg_simk = held.tile([P, 1], BF16, name="neg_simk")
-        nc.vector.tensor_scalar(neg_simk[:], simk_sb[:], -1.0, None, op0=ALU.mult)
-        neg_simq = held.tile([P, SLOTS], BF16, name="neg_simq")
-        nc.vector.tensor_scalar(neg_simq[:], simq_sb[:, 0:1].to_broadcast([P, SLOTS]), -1.0, None, op0=ALU.mult)
 
         warm = held.tile([P, 1], F32, name="warm")
         nc.vector.memset(warm[:], 0.0)
@@ -57,11 +53,11 @@ def tile_memory_kernel(tc, table, w, query, sim_q, sim_k, sim_b, offs, out):
         bias_sb = held.tile([P, 1], F32, name="bias_sb")
         nc.gpsimd.dma_start(bias_sb[:], sim_b.partition_broadcast(P))
 
-        def copy_from_bank(p, dst, src):
+        def copy_from_bank(p, dst, src, factor=1.0):
             if p % 2 == 1:
-                nc.scalar.activation(dst, src, FUNC.Copy)
+                nc.scalar.activation(dst, src, FUNC.Copy, scale=factor)
             else:
-                nc.vector.tensor_copy(dst, src)
+                nc.vector.tensor_scalar(dst, src, factor, None, op0=ALU.mult)
 
         kv_ps = []
         for p in range(PIECES):
@@ -76,26 +72,26 @@ def tile_memory_kernel(tc, table, w, query, sim_q, sim_k, sim_b, offs, out):
 
         logit_ps = logit_bank.tile([P, HALVES * SLOTS], F32, name="logit_ps")
         for p in range(PIECES):
-            kv_bf = held.tile([P, PIECE_BLOCKS[p] * P], BF16, name=f"kv_bf{p}")
-            copy_from_bank(p, kv_bf[:], kv_ps[p][:])
+            neg_kv = held.tile([P, PIECE_BLOCKS[p] * P], BF16, name=f"neg_kv{p}")
+            copy_from_bank(p, neg_kv[:], kv_ps[p][:], factor=-1.0)
             for b in range(PIECE_BLOCKS[p]):
                 t, h = divmod(FIRST_BLOCK[p] + b, HALVES)
                 col = h * SLOTS + t
                 nc.tensor.matmul(
                     logit_ps[:, col : col + 1],
-                    kv_bf[:, b * P : (b + 1) * P],
-                    neg_simk[:],
+                    neg_kv[:, b * P : (b + 1) * P],
+                    simk_sb[:],
                     start=(p == 0 and b == 0),
                     stop=False,
                 )
 
-        q_bf = held.tile([P, B], BF16, name="q_bf")
-        nc.vector.tensor_copy(q_bf[:], q_ps[:])
+        neg_q = held.tile([P, B], BF16, name="neg_q")
+        nc.vector.tensor_scalar(neg_q[:], q_ps[:], -1.0, None, op0=ALU.mult)
         for h in range(HALVES):
             nc.tensor.matmul(
                 logit_ps[:, h * SLOTS : (h + 1) * SLOTS],
-                q_bf[:, h * P : (h + 1) * P],
-                neg_simq[:],
+                neg_q[:, h * P : (h + 1) * P],
+                simq_sb[:, 0:1].to_broadcast([P, SLOTS]),
                 start=False,
                 stop=(h == HALVES - 1),
             )

@@ -4,7 +4,6 @@ from concourse.masks import make_identity
 BF16, F32, U16 = mybir.dt.bfloat16, mybir.dt.float32, mybir.dt.uint16
 ALU = mybir.AluOpType
 FUNC = mybir.ActivationFunctionType
-X = mybir.AxisListType.X
 
 P = 128
 S = 1024
@@ -17,6 +16,7 @@ GROUPS = N // (BANK_BLOCKS * P)
 PER_GROUP = BANK_BLOCKS // HALVES
 PIECE_BLOCKS = (4, 4, 4, 2, 1, 1)
 PIECES = len(PIECE_BLOCKS)
+VECTOR_PIECES = (0, 2)
 FIRST_BLOCK = tuple(sum(PIECE_BLOCKS[:k]) for k in range(PIECES))
 PSUM_BANKS = 8
 
@@ -54,7 +54,7 @@ def tile_memory_kernel(tc, table, w, query, sim_q, sim_k, sim_b, offs, out):
         nc.gpsimd.dma_start(bias_sb[:], sim_b.partition_broadcast(P))
 
         def copy_from_bank(p, dst, src, factor=1.0):
-            if p % 2 == 1:
+            if p not in VECTOR_PIECES:
                 nc.scalar.activation(dst, src, FUNC.Copy, scale=factor)
             else:
                 nc.vector.tensor_scalar(dst, src, factor, None, op0=ALU.mult)
@@ -98,13 +98,15 @@ def tile_memory_kernel(tc, table, w, query, sim_q, sim_k, sim_b, offs, out):
 
         kvT_ps = []
         for p in range(PIECES):
+            kv_sb = held.tile([P, PIECE_BLOCKS[p] * P], F32, name=f"kv_sb{p}")
             for b in range(PIECE_BLOCKS[p]):
+                if b % HALVES == 0:
+                    slot = slice(b * P, min(b + HALVES, PIECE_BLOCKS[p]) * P)
+                    copy_from_bank(p, kv_sb[:, slot], kv_ps[p][:, slot])
                 g, place = divmod(FIRST_BLOCK[p] + b, BANK_BLOCKS)
                 if place == 0:
                     kvT_ps.append(banks.tile([P, BANK_BLOCKS, P], F32, name=f"kvT_ps{g}", tag="bank"))
-                kv_sb = held.tile([P, P], F32, name=f"kv_sb{p}_{b}")
-                copy_from_bank(p, kv_sb[:], kv_ps[p][:, b * P : (b + 1) * P])
-                nc.tensor.transpose(kvT_ps[g][:, place, :], kv_sb[:], ident[:])
+                nc.tensor.transpose(kvT_ps[g][:, place, :], kv_sb[:, b * P : (b + 1) * P], ident[:])
 
         neg_logit = held.tile([P, HALVES, SLOTS], F32, name="neg_logit")
         neg_top = held.tile([P, HALVES], F32, name="neg_top")
@@ -127,8 +129,8 @@ def tile_memory_kernel(tc, table, w, query, sim_q, sim_k, sim_b, offs, out):
                 FUNC.Exp,
                 bias=neg_top[:, h : h + 1],
                 scale=-1.0,
+                accum_out=total[:, h : h + 1],
             )
-        nc.vector.tensor_reduce(total[:], expd[:], axis=X, op=ALU.add)
 
         inv_total = held.tile([P, HALVES], F32, name="inv_total")
         nc.vector.reciprocal(inv_total[:], total[:])

@@ -14,10 +14,11 @@ HALVES = B // P
 BANK_BLOCKS = 4
 GROUPS = N // (BANK_BLOCKS * P)
 PER_GROUP = BANK_BLOCKS // HALVES
-PIECE_BLOCKS = (4, 4, 4, 2, 1, 1)
+PIECE_BLOCKS = (4, 4, 3, 3, 1, 1)
 PIECES = len(PIECE_BLOCKS)
-VECTOR_PIECES = (0, 2)
 FIRST_BLOCK = tuple(sum(PIECE_BLOCKS[:k]) for k in range(PIECES))
+COPY_BLOCKS = 2
+EARLY_PIECES = 2
 PSUM_BANKS = 8
 
 FLOPS = 2 * P * P * (N + B) + 2 * P * (N + B) + 2 * P * N
@@ -54,7 +55,7 @@ def tile_memory_kernel(tc, table, w, query, sim_q, sim_k, sim_b, offs, out):
         nc.gpsimd.dma_start(bias_sb[:], sim_b.partition_broadcast(P))
 
         def copy_from_bank(p, dst, src, factor=1.0):
-            if p not in VECTOR_PIECES:
+            if p % 2 == 1:
                 nc.scalar.activation(dst, src, FUNC.Copy, scale=factor)
             else:
                 nc.vector.tensor_scalar(dst, src, factor, None, op0=ALU.mult)
@@ -71,6 +72,14 @@ def tile_memory_kernel(tc, table, w, query, sim_q, sim_k, sim_b, offs, out):
 
 
         logit_ps = logit_bank.tile([P, HALVES * SLOTS], F32, name="logit_ps")
+        kv_sb = []
+
+        def copy_unrounded(p):
+            kv_sb.append(held.tile([P, PIECE_BLOCKS[p] * P], F32, name=f"kv_sb{p}"))
+            for b in range(0, PIECE_BLOCKS[p], COPY_BLOCKS):
+                two = slice(b * P, min(b + COPY_BLOCKS, PIECE_BLOCKS[p]) * P)
+                copy_from_bank(p, kv_sb[p][:, two], kv_ps[p][:, two])
+
         for p in range(PIECES):
             neg_kv = held.tile([P, PIECE_BLOCKS[p] * P], BF16, name=f"neg_kv{p}")
             copy_from_bank(p, neg_kv[:], kv_ps[p][:], factor=-1.0)
@@ -84,6 +93,8 @@ def tile_memory_kernel(tc, table, w, query, sim_q, sim_k, sim_b, offs, out):
                     start=(p == 0 and b == 0),
                     stop=False,
                 )
+            if p < EARLY_PIECES:
+                copy_unrounded(p)
 
         neg_q = held.tile([P, B], BF16, name="neg_q")
         nc.vector.tensor_scalar(neg_q[:], q_ps[:], -1.0, None, op0=ALU.mult)
@@ -98,15 +109,13 @@ def tile_memory_kernel(tc, table, w, query, sim_q, sim_k, sim_b, offs, out):
 
         kvT_ps = []
         for p in range(PIECES):
-            kv_sb = held.tile([P, PIECE_BLOCKS[p] * P], F32, name=f"kv_sb{p}")
+            if p >= EARLY_PIECES:
+                copy_unrounded(p)
             for b in range(PIECE_BLOCKS[p]):
-                if b % HALVES == 0:
-                    slot = slice(b * P, min(b + HALVES, PIECE_BLOCKS[p]) * P)
-                    copy_from_bank(p, kv_sb[:, slot], kv_ps[p][:, slot])
                 g, place = divmod(FIRST_BLOCK[p] + b, BANK_BLOCKS)
                 if place == 0:
                     kvT_ps.append(banks.tile([P, BANK_BLOCKS, P], F32, name=f"kvT_ps{g}", tag="bank"))
-                nc.tensor.transpose(kvT_ps[g][:, place, :], kv_sb[:, b * P : (b + 1) * P], ident[:])
+                nc.tensor.transpose(kvT_ps[g][:, place, :], kv_sb[p][:, b * P : (b + 1) * P], ident[:])
 
         neg_logit = held.tile([P, HALVES, SLOTS], F32, name="neg_logit")
         neg_top = held.tile([P, HALVES], F32, name="neg_top")
@@ -139,8 +148,8 @@ def tile_memory_kernel(tc, table, w, query, sim_q, sim_k, sim_b, offs, out):
             nc.tensor.transpose(inv_ps[:, h * P : (h + 1) * P], inv_total[:, h : h + 1].to_broadcast([P, P]), ident[:])
 
         out_ps = [banks.tile([P, P], F32, name=f"out_ps{h}", tag="bank") for h in range(HALVES)]
-        for h in range(HALVES):
-            for p in range(0, GROUPS, 2):
+        for p in range(0, GROUPS, 2):
+            for h in range(HALVES):
                 for u in range(PER_GROUP):
                     b = u * HALVES + h
                     t_even, t_odd = p * PER_GROUP + u, (p + 1) * PER_GROUP + u

import concourse.mybir as mybir
from concourse.masks import make_identity

BF16, F32, U16 = mybir.dt.bfloat16, mybir.dt.float32, mybir.dt.uint16
ALU = mybir.AluOpType
FUNC = mybir.ActivationFunctionType

P = 128
S = 1024
SLOTS = 8
B = 256
N = SLOTS * B
HALVES = B // P
BANK_BLOCKS = 4
GROUPS = N // (BANK_BLOCKS * P)
PER_GROUP = BANK_BLOCKS // HALVES
PIECE_BLOCKS = (4, 4, 3, 3, 1, 1)
PIECES = len(PIECE_BLOCKS)
FIRST_BLOCK = tuple(sum(PIECE_BLOCKS[:k]) for k in range(PIECES))
COPY_BLOCKS = 2
EARLY_PIECES = 2
PSUM_BANKS = 8

FLOPS = 2 * P * P * (N + B) + 2 * P * (N + B) + 2 * P * N


def tile_memory_kernel(tc, table, w, query, sim_q, sim_k, sim_b, offs, out):
    nc = tc.nc
    with (
        tc.tile_pool(name="held", bufs=1) as held,
        tc.psum_pool(name="logit_bank", bufs=1) as logit_bank,
        tc.psum_pool(name="banks", bufs=PSUM_BANKS - 1) as banks,
    ):
        offsets = held.tile([P, N // 16], U16, name="offsets")
        nc.sync.dma_start(offsets[:], offs)
        table_sb = held.tile([P, S], BF16, name="table_sb")
        nc.scalar.dma_start(table_sb[:], table)
        w_sb = held.tile([P, P], BF16, name="w_sb")
        nc.sync.dma_start(w_sb[:], w)
        simk_sb = held.tile([P, 1], BF16, name="simk_sb")
        nc.scalar.dma_start(simk_sb[:], sim_k)
        simq_sb = held.tile([P, 1], BF16, name="simq_sb")
        nc.scalar.dma_start(simq_sb[:], sim_q)

        warm = held.tile([P, 1], F32, name="warm")
        nc.vector.memset(warm[:], 0.0)
        nc.scalar.activation(warm[:], warm[:], FUNC.Exp)

        ident = held.tile([P, P], F32, name="ident")
        make_identity(nc, ident[:])

        query_sb = held.tile([P, B], BF16, name="query_sb")
        nc.gpsimd.dma_start(query_sb[:], query)
        bias_sb = held.tile([P, 1], F32, name="bias_sb")
        nc.gpsimd.dma_start(bias_sb[:], sim_b.partition_broadcast(P))

        def copy_from_bank(p, dst, src, factor=1.0):
            if p % 2 == 1:
                nc.scalar.activation(dst, src, FUNC.Copy, scale=factor)
            else:
                nc.vector.tensor_scalar(dst, src, factor, None, op0=ALU.mult)

        kv_ps = []
        for p in range(PIECES):
            kv_ps.append(banks.tile([P, PIECE_BLOCKS[p] * P], F32, name=f"kv_ps{p}", tag="bank"))
            first_col = FIRST_BLOCK[p] * P // 16
            piece_offsets = offsets[:, first_col : first_col + PIECE_BLOCKS[p] * P // 16]
            nc.tensor.matmul(kv_ps[p][:], w_sb[:], table_sb[:].indirect(piece_offsets), start=True, stop=True)

        q_ps = banks.tile([P, B], BF16, name="q_ps", tag="bank")
        nc.tensor.matmul(q_ps[:], w_sb[:], query_sb[:], start=True, stop=True)


        logit_ps = logit_bank.tile([P, HALVES * SLOTS], F32, name="logit_ps")
        kv_sb = []

        def copy_unrounded(p):
            kv_sb.append(held.tile([P, PIECE_BLOCKS[p] * P], F32, name=f"kv_sb{p}"))
            for b in range(0, PIECE_BLOCKS[p], COPY_BLOCKS):
                two = slice(b * P, min(b + COPY_BLOCKS, PIECE_BLOCKS[p]) * P)
                copy_from_bank(p, kv_sb[p][:, two], kv_ps[p][:, two])

        for p in range(PIECES):
            neg_kv = held.tile([P, PIECE_BLOCKS[p] * P], BF16, name=f"neg_kv{p}")
            copy_from_bank(p, neg_kv[:], kv_ps[p][:], factor=-1.0)
            for b in range(PIECE_BLOCKS[p]):
                t, h = divmod(FIRST_BLOCK[p] + b, HALVES)
                col = h * SLOTS + t
                nc.tensor.matmul(
                    logit_ps[:, col : col + 1],
                    neg_kv[:, b * P : (b + 1) * P],
                    simk_sb[:],
                    start=(p == 0 and b == 0),
                    stop=False,
                )
            if p < EARLY_PIECES:
                copy_unrounded(p)

        neg_q = held.tile([P, B], BF16, name="neg_q")
        nc.vector.tensor_scalar(neg_q[:], q_ps[:], -1.0, None, op0=ALU.mult)
        for h in range(HALVES):
            nc.tensor.matmul(
                logit_ps[:, h * SLOTS : (h + 1) * SLOTS],
                neg_q[:, h * P : (h + 1) * P],
                simq_sb[:, 0:1].to_broadcast([P, SLOTS]),
                start=False,
                stop=(h == HALVES - 1),
            )

        kvT_ps = []
        for p in range(PIECES):
            if p >= EARLY_PIECES:
                copy_unrounded(p)
            for b in range(PIECE_BLOCKS[p]):
                g, place = divmod(FIRST_BLOCK[p] + b, BANK_BLOCKS)
                if place == 0:
                    kvT_ps.append(banks.tile([P, BANK_BLOCKS, P], F32, name=f"kvT_ps{g}", tag="bank"))
                nc.tensor.transpose(kvT_ps[g][:, place, :], kv_sb[p][:, b * P : (b + 1) * P], ident[:])

        neg_logit = held.tile([P, HALVES, SLOTS], F32, name="neg_logit")
        neg_top = held.tile([P, HALVES], F32, name="neg_top")
        expd = held.tile([P, HALVES, SLOTS], F32, name="expd")
        total = held.tile([P, HALVES], F32, name="total")
        for h in range(HALVES):
            nc.vector.tensor_scalar(
                neg_logit[:, h, :],
                logit_ps[:, h * SLOTS : (h + 1) * SLOTS],
                bias_sb[:, 0:1],
                None,
                op0=ALU.min,
                op1=ALU.min,
                accum_out=neg_top[:, h : h + 1],
            )
        for h in range(HALVES):
            nc.scalar.activation(
                expd[:, h, :],
                neg_logit[:, h, :],
                FUNC.Exp,
                bias=neg_top[:, h : h + 1],
                scale=-1.0,
                accum_out=total[:, h : h + 1],
            )

        inv_total = held.tile([P, HALVES], F32, name="inv_total")
        nc.vector.reciprocal(inv_total[:], total[:])
        inv_ps = banks.tile([P, B], F32, name="inv_ps", tag="bank")
        for h in range(HALVES):
            nc.tensor.transpose(inv_ps[:, h * P : (h + 1) * P], inv_total[:, h : h + 1].to_broadcast([P, P]), ident[:])

        out_ps = [banks.tile([P, P], F32, name=f"out_ps{h}", tag="bank") for h in range(HALVES)]
        for p in range(0, GROUPS, 2):
            for h in range(HALVES):
                for u in range(PER_GROUP):
                    b = u * HALVES + h
                    t_even, t_odd = p * PER_GROUP + u, (p + 1) * PER_GROUP + u
                    even_part = held.tile([P, P], F32, name=f"even_part{p}_{b}")
                    nc.scalar.activation(
                        even_part[:], kvT_ps[p][:, b, :], FUNC.Copy, scale=expd[:, h, t_even : t_even + 1]
                    )
                    pair_sum = held.tile([P, P], F32, name=f"pair_sum{p}_{b}")
                    nc.vector.scalar_tensor_tensor(
                        pair_sum[:],
                        kvT_ps[p + 1][:, b, :],
                        expd[:, h, t_odd : t_odd + 1],
                        even_part[:],
                        op0=ALU.mult,
                        op1=ALU.add,
                    )
                    nc.tensor.matmul(
                        out_ps[h][:],
                        pair_sum[:],
                        ident[:],
                        is_transpose=True,
                        start=(p == 0 and u == 0),
                        stop=(p == GROUPS - 2 and u == PER_GROUP - 1),
                    )

        inv_sb = held.tile([P, B], F32, name="inv_sb")
        nc.scalar.activation(inv_sb[:], inv_ps[:], FUNC.Copy)
        out_sb = held.tile([P, B], F32, name="out_sb")
        for h in range(HALVES):
            half = slice(h * P, (h + 1) * P)
            nc.vector.tensor_tensor(out_sb[:, half], out_ps[h][:], inv_sb[:, half], ALU.mult)
            nc.sync.dma_start(out[:, half], out_sb[:, half])
